import numpy as np
import ml_dtypes


def mxq(x, axis, fmt="e4m3"):
    dtype, down = {"e4m3": (ml_dtypes.float8_e4m3fn, 7), "e5m2": (ml_dtypes.float8_e5m2, 14)}[fmt]
    v = np.moveaxis(np.asarray(x, np.float32).astype(ml_dtypes.bfloat16).astype(np.float64), axis, -1)
    blocks = v.reshape(v.shape[:-1] + (-1, 32))
    amax = np.abs(blocks).max(-1, keepdims=True)
    byte = np.maximum(np.where(amax > 0, np.frexp(amax)[1] - 1 + 127, 0) - down, 1)
    scale = np.exp2(byte - 127.0)
    codes = (blocks / scale).astype(np.float32).astype(dtype).astype(np.float64)
    return np.moveaxis((codes * scale).reshape(v.shape), -1, axis)


WIDE = False


def mx_kscale(k):
    if not WIDE:
        return np.ones(k)
    levels = np.array([10, -10, 5, -5, 0])
    a = np.random.permutation(np.resize(levels, k // 512 * 4)).reshape(k // 512, 4)
    idx = np.arange(k)
    return np.exp2(a[idx // 512, idx % 128 // 32])


BF16 = ml_dtypes.bfloat16


def bf(x):
    return np.asarray(x, np.float32).astype(BF16)


def f64(x):
    return np.asarray(x).astype(np.float64)


E2M1 = np.array([0.0, 0.5, 1.0, 1.5, 2.0, 3.0, 4.0, 6.0, -0.0, -0.5, -1.0, -1.5, -2.0, -3.0, -4.0, -6.0])


def pack_weight(w, fmt):
    k, n = w.shape
    w = f64(bf(w)).reshape(k // 32, 32, n)
    amax = np.abs(w).max(1)
    if fmt == "e4m3":
        byte = np.frexp(amax)[1] - 1 + 127 - 7
    else:
        mant, ex = np.frexp(amax / 6.0)
        byte = np.where(mant > 0.5, ex, ex - 1) + 127
    byte = np.clip(np.where(amax > 0, byte, 1), 1, 254)
    scaled = (w * np.exp2(127.0 - byte)[:, None, :]).reshape(k, n).astype(np.float32)
    by_word = np.ascontiguousarray(scaled.reshape(k // 512, 128, 4, n).transpose(0, 1, 3, 2))
    if fmt == "e4m3":
        words = by_word.astype(ml_dtypes.float8_e4m3fn).view(np.uint8)
    else:
        c = by_word.astype(ml_dtypes.float4_e2m1fn).view(np.uint8) & 0xF
        words = c[..., 0::2] | (c[..., 1::2] << 4)
    return np.ascontiguousarray(words), np.ascontiguousarray(byte.astype(np.uint8).reshape(k // 512, 16, n))


def unpack_weight(words, scales, fmt):
    g, p, n, _ = words.shape
    if fmt == "e4m3":
        vals = np.ascontiguousarray(words).view(ml_dtypes.float8_e4m3fn).astype(np.float64)
    else:
        nib = np.empty((g, p, n, 4), np.uint8)
        nib[..., 0::2] = words & 0xF
        nib[..., 1::2] = words >> 4
        vals = E2M1[nib]
    vals = vals * np.repeat(np.exp2(scales.astype(np.float64) - 127.0), 8, axis=1)[..., None]
    return vals.transpose(0, 1, 3, 2).reshape(g * 512, n)


BS, N, D, B, D_PM = 2, 1024, 1024, 8, 512


def setup_inputs():
    k, t = mx_kscale(D_PM), mx_kscale(D_PM)
    w = np.eye(D_PM) / B + 1.6 / np.sqrt(B * D_PM) * np.random.standard_normal((BS, B, D_PM, D_PM))
    pre = bf(np.random.standard_normal((BS, N, D_PM)) * k)
    W_pm = bf(w * t[:, None] / k)
    proj = np.random.standard_normal((D, D_PM)) / np.sqrt(D_PM) / t
    words, scales = pack_weight(proj.T, "e4m3")
    proj_out_b = bf(np.random.standard_normal(D) * 0.3)
    return {"pre": pre,
            "W_pm": W_pm,
            "proj_out_w_words": words,
            "proj_out_w_scales": scales,
            "proj_out_b": proj_out_b}


def reference(pre, W_pm, proj_out_w_words, proj_out_w_scales, proj_out_b):
    W_sum = np.sum(f64(W_pm), axis=1)
    post = mxq(f64(pre), 2, "e4m3") @ mxq(W_sum, 2, "e4m3").transpose(0, 2, 1)
    return (mxq(post, 2, "e4m3") @ unpack_weight(proj_out_w_words, proj_out_w_scales, "e4m3")) + f64(proj_out_b)

@@ -1,0 +1,237 @@
+from contextlib import ExitStack
+
+import concourse.mybir as mybir
+from concourse.masks import make_identity
+
+FLOPS = 2 * 2 * 1024 * 512 * 512 + 2 * 2 * 1024 * 512 * 1024
+
+FP8X4 = mybir.dt.float8_e4m3fn_x4
+BF16 = mybir.dt.bfloat16
+F32 = mybir.dt.float32
+I32 = mybir.dt.int32
+U32 = mybir.dt.uint32
+U8 = mybir.dt.uint8
+ADD = mybir.AluOpType.add
+
+P = 128
+PACK = 4
+SAMPLES = 2
+TOKENS = 1024
+MEM = 512
+FEAT = 1024
+BANKS = 8
+BLOCKS = TOKENS // P
+HALF = 512
+ROW_GROUPS = P // BANKS
+ROWS = MEM // ROW_GROUPS
+CHUNK_ROWS = 8
+CHUNKS = ROWS // CHUNK_ROWS
+
+
+def tile_proceduralmemory_pc_kernel(
+    tc, pre, W_pm, proj_out_w_words, proj_out_w_scales, proj_out_b, out
+):
+    nc = tc.nc
+    with ExitStack() as ctx:
+        consts = ctx.enter_context(tc.tile_pool(name="consts", bufs=1))
+        sample = ctx.enter_context(tc.tile_pool(name="sample", bufs=SAMPLES))
+        banks = ctx.enter_context(tc.tile_pool(name="banks", bufs=SAMPLES * CHUNKS))
+        work = ctx.enter_context(tc.tile_pool(name="work", bufs=3))
+        results = ctx.enter_context(tc.tile_pool(name="results", bufs=SAMPLES * BLOCKS))
+        psum = ctx.enter_context(tc.psum_pool(name="psum", bufs=2))
+
+        ident = consts.tile([P, P], BF16)
+        make_identity(nc, ident[:])
+        fold_f32 = consts.tile([P, ROW_GROUPS], F32)
+        nc.vector.tensor_reduce(
+            out=fold_f32[:],
+            in_=ident[:].rearrange("q (k r) -> q r k", r=ROW_GROUPS),
+            axis=mybir.AxisListType.X,
+            op=ADD,
+        )
+        fold = consts.tile([P, ROW_GROUPS], BF16)
+        nc.vector.tensor_copy(out=fold[:], in_=fold_f32[:])
+        ones = consts.tile([P, P], BF16)
+        nc.vector.memset(ones[:], 1.0)
+        bias_row = consts.tile([P, FEAT], BF16)
+        nc.vector.memset(bias_row[:], 0.0)
+        bias_all = consts.tile([P, FEAT], F32)
+        w_words = consts.tile([P, FEAT], U32, align_bytes=64)
+        w_scales = consts.tile([P, FEAT], U8, align_bytes=64)
+        nc.vector.memset(w_scales[:].bitcast(I32), 0)
+
+        pre_rows = []
+        bank_rows = []
+
+        def load_sample(b):
+            pre_tile = sample.tile([P, BLOCKS, MEM], BF16)
+            nc.sync.dma_start(
+                out=pre_tile[:], in_=pre[b].rearrange("(p nb) j -> p nb j", nb=BLOCKS)
+            )
+            pre_rows.append(pre_tile)
+            rows_view = W_pm[b].rearrange("k (r s) j -> (k r) s j", s=ROWS)
+            chunks = []
+            for c in range(CHUNKS):
+                chunk_tile = banks.tile([P, CHUNK_ROWS, MEM], BF16)
+                nc.sync.dma_start(
+                    out=chunk_tile[:],
+                    in_=rows_view[:, c * CHUNK_ROWS : (c + 1) * CHUNK_ROWS, :],
+                )
+                chunks.append(chunk_tile)
+            bank_rows.append(chunks)
+
+        load_sample(0)
+        nc.sync.dma_start(
+            out=bias_row[0:1, :], in_=proj_out_b.rearrange("(o d) -> o d", o=1)
+        )
+        nc.sync.dma_start(
+            out=w_words[:].bitcast(I32),
+            in_=proj_out_w_words[0].rearrange("p n t -> p (n t)").bitcast(I32),
+        )
+        for quadrant in range(4):
+            nc.sync.dma_start(
+                out=w_scales[32 * quadrant : 32 * quadrant + 4, :].bitcast(I32),
+                in_=proj_out_w_scales[0, 4 * quadrant : 4 * quadrant + 4, :].bitcast(I32),
+            )
+        load_sample(1)
+
+        pre_codes = []
+        pre_scales = []
+        wsum_grouped = []
+        wsum_codes = []
+        wsum_scales = []
+
+        def quantise_tokens(b):
+            grouped = sample.tile([P, BLOCKS, P, PACK], BF16, align_bytes=64)
+            for nb in range(BLOCKS):
+                flipped = psum.tile([P, PACK, P], BF16)
+                for t in range(PACK):
+                    nc.tensor.transpose(
+                        out=flipped[:, t, :],
+                        in_=pre_rows[b][:, nb, t * P : (t + 1) * P],
+                        identity=ident[:],
+                    )
+                nc.scalar.copy(
+                    out=grouped[:, nb, :, :], in_=flipped[:].rearrange("p t n -> p n t")
+                )
+            codes = sample.tile([P, TOKENS], U32, align_bytes=64)
+            scales = sample.tile([P, TOKENS], U8, align_bytes=64)
+            nc.vector.quantize_mx(
+                out=codes[:].bitcast(FP8X4),
+                scales=scales[:],
+                in_=grouped[:].rearrange("p nb n t -> p (nb n t)"),
+            )
+            pre_codes.append(codes)
+            pre_scales.append(scales)
+
+        def start_bank_sums(b):
+            grouped_sums = sample.tile(
+                [P, PACK, ROW_GROUPS, ROWS // PACK, PACK], BF16, align_bytes=64
+            )
+            wsum_grouped.append(grouped_sums)
+
+        def sum_banks(b, c):
+            sums = psum.tile([P, PACK, ROW_GROUPS, CHUNK_ROWS // PACK, PACK], F32)
+            for s in range(CHUNK_ROWS):
+                for t in range(PACK):
+                    nc.tensor.matmul(
+                        out=sums[:, s % PACK, :, s // PACK, t],
+                        lhsT=bank_rows[b][c][:, s, t * P : (t + 1) * P],
+                        rhs=fold[:],
+                        start=True,
+                        stop=True,
+                    )
+            per_chunk = CHUNK_ROWS // PACK
+            nc.scalar.copy(
+                out=wsum_grouped[b][:].rearrange("p T r s t -> p (T r) s t")[
+                    :, :, c * per_chunk : (c + 1) * per_chunk, :
+                ],
+                in_=sums[:].rearrange("p T r s t -> p (T r) s t"),
+            )
+
+        def quantise_bank_sums(b):
+            codes_w = sample.tile([P, MEM], U32, align_bytes=64)
+            scales_w = sample.tile([P, MEM], U8, align_bytes=64)
+            nc.vector.quantize_mx(
+                out=codes_w[:].bitcast(FP8X4),
+                scales=scales_w[:],
+                in_=wsum_grouped[b][:].rearrange("p T r s t -> p (T r s t)"),
+            )
+            wsum_codes.append(codes_w)
+            wsum_scales.append(scales_w)
+
+        def spread_bias():
+            for h in range(FEAT // HALF):
+                cols = slice(h * HALF, (h + 1) * HALF)
+                product = psum.tile([P, HALF], F32)
+                nc.tensor.matmul(
+                    out=product[:], lhsT=ones[:], rhs=bias_row[:, cols], start=True, stop=True
+                )
+                nc.scalar.copy(out=bias_all[:, cols], in_=product[:])
+
+        def first_product(b, nb):
+            post = psum.tile([P, PACK, P], F32)
+            tokens = slice(nb * P, (nb + 1) * P)
+            for T in range(PACK):
+                rows = slice(T * P, (T + 1) * P)
+                nc.tensor.matmul_mx(
+                    out=post[:, T, :],
+                    lhsT=wsum_codes[b][:, rows].bitcast(FP8X4),
+                    lhsT_scale=wsum_scales[b][:, rows],
+                    rhs=pre_codes[b][:, tokens].bitcast(FP8X4),
+                    rhs_scale=pre_scales[b][:, tokens],
+                    start=True,
+                    stop=True,
+                )
+            post_grouped = work.tile([P, P, PACK], BF16, align_bytes=64)
+            nc.scalar.copy(out=post_grouped[:], in_=post[:].rearrange("p T n -> p n T"))
+            post_codes = work.tile([P, P], U32, align_bytes=64)
+            post_scales = work.tile([P, P], U8, align_bytes=64)
+            nc.vector.quantize_mx(
+                out=post_codes[:].bitcast(FP8X4),
+                scales=post_scales[:],
+                in_=post_grouped[:].rearrange("p n T -> p (n T)"),
+            )
+            return post_codes, post_scales
+
+        def second_product(b, nb, post_codes, post_scales):
+            result = results.tile([P, FEAT], F32)
+            for h in range(FEAT // HALF):
+                cols = slice(h * HALF, (h + 1) * HALF)
+                product = psum.tile([P, HALF], F32)
+                nc.tensor.matmul_mx(
+                    out=product[:],
+                    lhsT=post_codes[:].bitcast(FP8X4),
+                    lhsT_scale=post_scales[:],
+                    rhs=w_words[:, cols].bitcast(FP8X4),
+                    rhs_scale=w_scales[:, cols],
+                    start=True,
+                    stop=True,
+                )
+                nc.vector.tensor_tensor(
+                    out=result[:, cols], in0=product[:], in1=bias_all[:, cols], op=ADD
+                )
+            nc.sync.dma_start(
+                out=out[b].rearrange("(p nb) d -> p nb d", nb=BLOCKS)[:, nb, :], in_=result[:]
+            )
+
+        quantise_tokens(0)
+        start_bank_sums(0)
+        for c in range(CHUNKS):
+            sum_banks(0, c)
+        quantise_bank_sums(0)
+        spread_bias()
+        quantise_tokens(1)
+        start_bank_sums(1)
+
+        blocks = [(b, nb) for b in range(SAMPLES) for nb in range(BLOCKS)]
+        quantised = first_product(0, 0)
+        for step, (b, nb) in enumerate(blocks):
+            if step < CHUNKS:
+                sum_banks(1, step)
+            if step == CHUNKS:
+                quantise_bank_sums(1)
+            current = quantised
+            if step + 1 < len(blocks):
+                quantised = first_product(*blocks[step + 1])
+            second_product(b, nb, *current)

@@ -26,6 +26,7 @@ ROW_GROUPS = P // BANKS
 ROWS = MEM // ROW_GROUPS
 CHUNK_ROWS = 8
 CHUNKS = ROWS // CHUNK_ROWS
+HALF_BLOCKS = BLOCKS // 2
 
 
 def tile_proceduralmemory_pc_kernel(
@@ -33,13 +34,25 @@ def tile_proceduralmemory_pc_kernel(
 ):
     nc = tc.nc
     with ExitStack() as ctx:
+        ctx.enter_context(tc.manual_schedule())
         consts = ctx.enter_context(tc.tile_pool(name="consts", bufs=1))
         sample = ctx.enter_context(tc.tile_pool(name="sample", bufs=SAMPLES))
+        halves = ctx.enter_context(tc.tile_pool(name="halves", bufs=2 * SAMPLES))
         banks = ctx.enter_context(tc.tile_pool(name="banks", bufs=SAMPLES * CHUNKS))
-        work = ctx.enter_context(tc.tile_pool(name="work", bufs=3))
+        work = ctx.enter_context(tc.tile_pool(name="work", bufs=4))
         results = ctx.enter_context(tc.tile_pool(name="results", bufs=SAMPLES * BLOCKS))
-        psum = ctx.enter_context(tc.psum_pool(name="psum", bufs=2))
+        psum_early = ctx.enter_context(tc.psum_pool(name="psum_early", bufs=2))
+        psum_post = ctx.enter_context(tc.psum_pool(name="psum_post", bufs=2))
+        psum_product = ctx.enter_context(tc.psum_pool(name="psum_product", bufs=4))
 
+        ones = consts.tile([P, P], BF16)
+        nc.vector.memset(ones[:], 1.0)
+        bias_row = consts.tile([P, FEAT], BF16)
+        nc.vector.memset(bias_row[:], 0.0)
+        bias_all = consts.tile([P, FEAT], F32)
+        w_words = consts.tile([P, FEAT], U32, align_bytes=64)
+        w_scales = consts.tile([P, FEAT], U8, align_bytes=64)
+        nc.vector.memset(w_scales[:].bitcast(I32), 0)
         ident = consts.tile([P, P], BF16)
         make_identity(nc, ident[:])
         fold_f32 = consts.tile([P, ROW_GROUPS], F32)
@@ -51,39 +64,35 @@ def tile_proceduralmemory_pc_kernel(
         )
         fold = consts.tile([P, ROW_GROUPS], BF16)
         nc.vector.tensor_copy(out=fold[:], in_=fold_f32[:])
-        ones = consts.tile([P, P], BF16)
-        nc.vector.memset(ones[:], 1.0)
-        bias_row = consts.tile([P, FEAT], BF16)
-        nc.vector.memset(bias_row[:], 0.0)
-        bias_all = consts.tile([P, FEAT], F32)
-        w_words = consts.tile([P, FEAT], U32, align_bytes=64)
-        w_scales = consts.tile([P, FEAT], U8, align_bytes=64)
-        nc.vector.memset(w_scales[:].bitcast(I32), 0)
 
-        pre_rows = []
-        bank_rows = []
+        pre_rows = {}
+        bank_rows = {}
 
-        def load_sample(b):
-            pre_tile = sample.tile([P, BLOCKS, MEM], BF16)
-            nc.sync.dma_start(
-                out=pre_tile[:], in_=pre[b].rearrange("(p nb) j -> p nb j", nb=BLOCKS)
-            )
-            pre_rows.append(pre_tile)
+        def load_tokens(b):
+            tokens_view = pre[b].rearrange("(p nb) j -> p nb j", nb=BLOCKS)
+            for half in range(2):
+                pre_tile = halves.tile([P, HALF_BLOCKS, MEM], BF16)
+                nc.sync.dma_start(
+                    out=pre_tile[:],
+                    in_=tokens_view[:, half * HALF_BLOCKS : (half + 1) * HALF_BLOCKS, :],
+                )
+                pre_rows[(b, half)] = pre_tile
+
+        def load_banks(b):
             rows_view = W_pm[b].rearrange("k (r s) j -> (k r) s j", s=ROWS)
-            chunks = []
             for c in range(CHUNKS):
                 chunk_tile = banks.tile([P, CHUNK_ROWS, MEM], BF16)
                 nc.sync.dma_start(
                     out=chunk_tile[:],
                     in_=rows_view[:, c * CHUNK_ROWS : (c + 1) * CHUNK_ROWS, :],
                 )
-                chunks.append(chunk_tile)
-            bank_rows.append(chunks)
+                bank_rows[(b, c)] = chunk_tile
 
-        load_sample(0)
+        load_tokens(0)
         nc.sync.dma_start(
             out=bias_row[0:1, :], in_=proj_out_b.rearrange("(o d) -> o d", o=1)
         )
+        load_banks(0)
         nc.sync.dma_start(
             out=w_words[:].bitcast(I32),
             in_=proj_out_w_words[0].rearrange("p n t -> p (n t)").bitcast(I32),
@@ -93,50 +102,56 @@ def tile_proceduralmemory_pc_kernel(
                 out=w_scales[32 * quadrant : 32 * quadrant + 4, :].bitcast(I32),
                 in_=proj_out_w_scales[0, 4 * quadrant : 4 * quadrant + 4, :].bitcast(I32),
             )
-        load_sample(1)
+        load_tokens(1)
+        load_banks(1)
 
-        pre_codes = []
-        pre_scales = []
-        wsum_grouped = []
-        wsum_codes = []
-        wsum_scales = []
-
-        def quantise_tokens(b):
-            grouped = sample.tile([P, BLOCKS, P, PACK], BF16, align_bytes=64)
-            for nb in range(BLOCKS):
-                flipped = psum.tile([P, PACK, P], BF16)
-                for t in range(PACK):
-                    nc.tensor.transpose(
-                        out=flipped[:, t, :],
-                        in_=pre_rows[b][:, nb, t * P : (t + 1) * P],
-                        identity=ident[:],
-                    )
-                nc.scalar.copy(
-                    out=grouped[:, nb, :, :], in_=flipped[:].rearrange("p t n -> p n t")
-                )
+        pre_codes = {}
+        pre_scales = {}
+        wsum_grouped = {}
+        wsum_codes = {}
+        wsum_scales = {}
+        for b in range(SAMPLES):
             codes = sample.tile([P, TOKENS], U32, align_bytes=64)
             scales = sample.tile([P, TOKENS], U8, align_bytes=64)
-            nc.vector.quantize_mx(
-                out=codes[:].bitcast(FP8X4),
-                scales=scales[:],
-                in_=grouped[:].rearrange("p nb n t -> p (nb n t)"),
-            )
-            pre_codes.append(codes)
-            pre_scales.append(scales)
-
-        def start_bank_sums(b):
             grouped_sums = sample.tile(
                 [P, PACK, ROW_GROUPS, ROWS // PACK, PACK], BF16, align_bytes=64
             )
-            wsum_grouped.append(grouped_sums)
+            codes_w = sample.tile([P, MEM], U32, align_bytes=64)
+            scales_w = sample.tile([P, MEM], U8, align_bytes=64)
+            pre_codes[b] = codes
+            pre_scales[b] = scales
+            wsum_grouped[b] = grouped_sums
+            wsum_codes[b] = codes_w
+            wsum_scales[b] = scales_w
+
+        def quantise_tokens(b, half):
+            grouped = halves.tile([P, HALF_BLOCKS, P, PACK], BF16, align_bytes=64)
+            for nb in range(HALF_BLOCKS):
+                flipped = psum_early.tile([P, PACK, P], BF16, tag="early")
+                for t in range(PACK):
+                    nc.tensor.transpose(
+                        out=flipped[:, t, :],
+                        in_=pre_rows[(b, half)][:, nb, t * P : (t + 1) * P],
+                        identity=ident[:],
+                    )
+                copy = nc.scalar.copy if nb % 2 == 0 else nc.vector.tensor_copy
+                copy(out=grouped[:, nb, :, :], in_=flipped[:].rearrange("p t n -> p n t"))
+            cols = slice(half * HALF_BLOCKS * P, (half + 1) * HALF_BLOCKS * P)
+            nc.vector.quantize_mx(
+                out=pre_codes[b][:, cols].bitcast(FP8X4),
+                scales=pre_scales[b][:, cols],
+                in_=grouped[:].rearrange("p nb n t -> p (nb n t)"),
+            )
 
         def sum_banks(b, c):
-            sums = psum.tile([P, PACK, ROW_GROUPS, CHUNK_ROWS // PACK, PACK], F32)
+            sums = psum_early.tile(
+                [P, PACK, ROW_GROUPS, CHUNK_ROWS // PACK, PACK], F32, tag="early"
+            )
             for s in range(CHUNK_ROWS):
                 for t in range(PACK):
                     nc.tensor.matmul(
                         out=sums[:, s % PACK, :, s // PACK, t],
-                        lhsT=bank_rows[b][c][:, s, t * P : (t + 1) * P],
+                        lhsT=bank_rows[(b, c)][:, s, t * P : (t + 1) * P],
                         rhs=fold[:],
                         start=True,
                         stop=True,
@@ -150,27 +165,29 @@ def tile_proceduralmemory_pc_kernel(
             )
 
         def quantise_bank_sums(b):
-            codes_w = sample.tile([P, MEM], U32, align_bytes=64)
-            scales_w = sample.tile([P, MEM], U8, align_bytes=64)
             nc.vector.quantize_mx(
-                out=codes_w[:].bitcast(FP8X4),
-                scales=scales_w[:],
+                out=wsum_codes[b][:].bitcast(FP8X4),
+                scales=wsum_scales[b][:],
                 in_=wsum_grouped[b][:].rearrange("p T r s t -> p (T r s t)"),
             )
-            wsum_codes.append(codes_w)
-            wsum_scales.append(scales_w)
 
         def spread_bias():
             for h in range(FEAT // HALF):
                 cols = slice(h * HALF, (h + 1) * HALF)
-                product = psum.tile([P, HALF], F32)
+                product = psum_product.tile([P, HALF], F32)
                 nc.tensor.matmul(
                     out=product[:], lhsT=ones[:], rhs=bias_row[:, cols], start=True, stop=True
                 )
                 nc.scalar.copy(out=bias_all[:, cols], in_=product[:])
 
-        def first_product(b, nb):
-            post = psum.tile([P, PACK, P], F32)
+        post_grouped = {}
+        post_codes = {}
+        post_scales = {}
+        products = {}
+
+        def first_product(g):
+            b, nb = divmod(g, BLOCKS)
+            post = psum_post.tile([P, PACK, P], F32)
             tokens = slice(nb * P, (nb + 1) * P)
             for T in range(PACK):
                 rows = slice(T * P, (T + 1) * P)
@@ -183,55 +200,68 @@ def tile_proceduralmemory_pc_kernel(
                     start=True,
                     stop=True,
                 )
-            post_grouped = work.tile([P, P, PACK], BF16, align_bytes=64)
-            nc.scalar.copy(out=post_grouped[:], in_=post[:].rearrange("p T n -> p n T"))
-            post_codes = work.tile([P, P], U32, align_bytes=64)
-            post_scales = work.tile([P, P], U8, align_bytes=64)
-            nc.vector.quantize_mx(
-                out=post_codes[:].bitcast(FP8X4),
-                scales=post_scales[:],
-                in_=post_grouped[:].rearrange("p n T -> p (n T)"),
-            )
-            return post_codes, post_scales
+            grouped_post = work.tile([P, P, PACK], BF16, align_bytes=64)
+            nc.scalar.copy(out=grouped_post[:], in_=post[:].rearrange("p T n -> p n T"))
+            post_grouped[g] = grouped_post
 
-        def second_product(b, nb, post_codes, post_scales):
-            result = results.tile([P, FEAT], F32)
+        def quantise_post(g):
+            codes_p = work.tile([P, P], U32, align_bytes=64)
+            scales_p = work.tile([P, P], U8, align_bytes=64)
+            nc.vector.quantize_mx(
+                out=codes_p[:].bitcast(FP8X4),
+                scales=scales_p[:],
+                in_=post_grouped[g][:].rearrange("p n T -> p (n T)"),
+            )
+            post_codes[g] = codes_p
+            post_scales[g] = scales_p
+
+        def second_product(g):
             for h in range(FEAT // HALF):
                 cols = slice(h * HALF, (h + 1) * HALF)
-                product = psum.tile([P, HALF], F32)
+                product = psum_product.tile([P, HALF], F32)
                 nc.tensor.matmul_mx(
                     out=product[:],
-                    lhsT=post_codes[:].bitcast(FP8X4),
-                    lhsT_scale=post_scales[:],
+                    lhsT=post_codes[g][:].bitcast(FP8X4),
+                    lhsT_scale=post_scales[g][:],
                     rhs=w_words[:, cols].bitcast(FP8X4),
                     rhs_scale=w_scales[:, cols],
                     start=True,
                     stop=True,
                 )
+                products[(g, h)] = product
+
+        def add_bias_and_store(g):
+            b, nb = divmod(g, BLOCKS)
+            result = results.tile([P, FEAT], F32)
+            for h in range(FEAT // HALF):
+                cols = slice(h * HALF, (h + 1) * HALF)
                 nc.vector.tensor_tensor(
-                    out=result[:, cols], in0=product[:], in1=bias_all[:, cols], op=ADD
+                    out=result[:, cols], in0=products[(g, h)][:], in1=bias_all[:, cols], op=ADD
                 )
             nc.sync.dma_start(
                 out=out[b].rearrange("(p nb) d -> p nb d", nb=BLOCKS)[:, nb, :], in_=result[:]
             )
 
-        quantise_tokens(0)
-        start_bank_sums(0)
+        quantise_tokens(0, 0)
+        quantise_tokens(0, 1)
         for c in range(CHUNKS):
             sum_banks(0, c)
         quantise_bank_sums(0)
         spread_bias()
-        quantise_tokens(1)
-        start_bank_sums(1)
 
-        blocks = [(b, nb) for b in range(SAMPLES) for nb in range(BLOCKS)]
-        quantised = first_product(0, 0)
-        for step, (b, nb) in enumerate(blocks):
-            if step < CHUNKS:
+        n_blocks = SAMPLES * BLOCKS
+        for step in range(-2, n_blocks):
+            if step + 2 < n_blocks:
+                first_product(step + 2)
+            if 0 <= step + 1 < n_blocks:
+                second_product(step + 1)
+            if step >= 0:
+                add_bias_and_store(step)
+            if step + 2 < n_blocks:
+                quantise_post(step + 2)
+            if step < 0:
+                quantise_tokens(1, step + 2)
+            elif step < CHUNKS:
                 sum_banks(1, step)
-            if step == CHUNKS:
+            elif step == CHUNKS:
                 quantise_bank_sums(1)
-            current = quantised
-            if step + 1 < len(blocks):
-                quantised = first_product(*blocks[step + 1])
-            second_product(b, nb, *current)

@@ -26,6 +26,7 @@ ROW_GROUPS = P // BANKS
 ROWS = MEM // ROW_GROUPS
 CHUNK_ROWS = 8
 CHUNKS = ROWS // CHUNK_ROWS
+GPSIMD_SHARE = 3
 HALF_BLOCKS = BLOCKS // 2
 
 
@@ -235,9 +236,15 @@ def tile_proceduralmemory_pc_kernel(
             result = results.tile([P, FEAT], F32)
             for h in range(FEAT // HALF):
                 cols = slice(h * HALF, (h + 1) * HALF)
-                nc.vector.tensor_tensor(
-                    out=result[:, cols], in0=products[(g, h)][:], in1=bias_all[:, cols], op=ADD
-                )
+                if (2 * g + h) % GPSIMD_SHARE == GPSIMD_SHARE - 1:
+                    nc.scalar.copy(out=result[:, cols], in_=products[(g, h)][:])
+                    nc.gpsimd.tensor_tensor(
+                        out=result[:, cols], in0=result[:, cols], in1=bias_all[:, cols], op=ADD
+                    )
+                else:
+                    nc.vector.tensor_tensor(
+                        out=result[:, cols], in0=products[(g, h)][:], in1=bias_all[:, cols], op=ADD
+                    )
             nc.sync.dma_start(
                 out=out[b].rearrange("(p nb) d -> p nb d", nb=BLOCKS)[:, nb, :], in_=result[:]
             )

@@ -22,11 +22,11 @@ FEAT = 1024
 BANKS = 8
 BLOCKS = TOKENS // P
 HALF = 512
-ROW_GROUPS = P // BANKS
+BANK_SETS = 2
+SET_BANKS = BANKS // BANK_SETS
+ROW_GROUPS = P // SET_BANKS
 ROWS = MEM // ROW_GROUPS
-CHUNK_ROWS = 8
-CHUNKS = ROWS // CHUNK_ROWS
-GPSIMD_SHARE = 3
+CHUNKS = ROWS // PACK
 HALF_BLOCKS = BLOCKS // 2
 
 
@@ -80,12 +80,13 @@ def tile_proceduralmemory_pc_kernel(
                 pre_rows[(b, half)] = pre_tile
 
         def load_banks(b):
-            rows_view = W_pm[b].rearrange("k (r s) j -> (k r) s j", s=ROWS)
+            rows_view = W_pm[b].rearrange(
+                "(h k) (r s) j -> (k r) h s j", h=BANK_SETS, s=ROWS
+            )
             for c in range(CHUNKS):
-                chunk_tile = banks.tile([P, CHUNK_ROWS, MEM], BF16)
+                chunk_tile = banks.tile([P, BANK_SETS, PACK, MEM], BF16)
                 nc.sync.dma_start(
-                    out=chunk_tile[:],
-                    in_=rows_view[:, c * CHUNK_ROWS : (c + 1) * CHUNK_ROWS, :],
+                    out=chunk_tile[:], in_=rows_view[:, :, c * PACK : (c + 1) * PACK, :]
                 )
                 bank_rows[(b, c)] = chunk_tile
 
@@ -115,7 +116,7 @@ def tile_proceduralmemory_pc_kernel(
             codes = sample.tile([P, TOKENS], U32, align_bytes=64)
             scales = sample.tile([P, TOKENS], U8, align_bytes=64)
             grouped_sums = sample.tile(
-                [P, PACK, ROW_GROUPS, ROWS // PACK, PACK], BF16, align_bytes=64
+                [P, PACK, ROW_GROUPS, CHUNKS, PACK], BF16, align_bytes=64
             )
             codes_w = sample.tile([P, MEM], U32, align_bytes=64)
             scales_w = sample.tile([P, MEM], U8, align_bytes=64)
@@ -145,31 +146,27 @@ def tile_proceduralmemory_pc_kernel(
             )
 
         def sum_banks(b, c):
-            sums = psum_early.tile(
-                [P, PACK, ROW_GROUPS, CHUNK_ROWS // PACK, PACK], F32, tag="early"
-            )
-            for s in range(CHUNK_ROWS):
+            sums = psum_early.tile([P, PACK, ROW_GROUPS, PACK], F32, tag="early")
+            for T in range(PACK):
                 for t in range(PACK):
-                    nc.tensor.matmul(
-                        out=sums[:, s % PACK, :, s // PACK, t],
-                        lhsT=bank_rows[(b, c)][:, s, t * P : (t + 1) * P],
-                        rhs=fold[:],
-                        start=True,
-                        stop=True,
-                    )
-            per_chunk = CHUNK_ROWS // PACK
+                    for h in range(BANK_SETS):
+                        nc.tensor.matmul(
+                            out=sums[:, T, :, t],
+                            lhsT=bank_rows[(b, c)][:, h, T, t * P : (t + 1) * P],
+                            rhs=fold[:],
+                            start=(h == 0),
+                            stop=(h == BANK_SETS - 1),
+                        )
             nc.scalar.copy(
-                out=wsum_grouped[b][:].rearrange("p T r s t -> p (T r) s t")[
-                    :, :, c * per_chunk : (c + 1) * per_chunk, :
-                ],
-                in_=sums[:].rearrange("p T r s t -> p (T r) s t"),
+                out=wsum_grouped[b][:].rearrange("p T r c t -> p (T r) c t")[:, :, c, :],
+                in_=sums[:].rearrange("p T r t -> p (T r) t"),
             )
 
         def quantise_bank_sums(b):
             nc.vector.quantize_mx(
                 out=wsum_codes[b][:].bitcast(FP8X4),
                 scales=wsum_scales[b][:],
-                in_=wsum_grouped[b][:].rearrange("p T r s t -> p (T r s t)"),
+                in_=wsum_grouped[b][:].rearrange("p T r c t -> p (T r c t)"),
             )
 
         def spread_bias():
@@ -236,15 +233,9 @@ def tile_proceduralmemory_pc_kernel(
             result = results.tile([P, FEAT], F32)
             for h in range(FEAT // HALF):
                 cols = slice(h * HALF, (h + 1) * HALF)
-                if (2 * g + h) % GPSIMD_SHARE == GPSIMD_SHARE - 1:
-                    nc.scalar.copy(out=result[:, cols], in_=products[(g, h)][:])
-                    nc.gpsimd.tensor_tensor(
-                        out=result[:, cols], in0=result[:, cols], in1=bias_all[:, cols], op=ADD
-                    )
-                else:
-                    nc.vector.tensor_tensor(
-                        out=result[:, cols], in0=products[(g, h)][:], in1=bias_all[:, cols], op=ADD
-                    )
+                nc.vector.tensor_tensor(
+                    out=result[:, cols], in0=products[(g, h)][:], in1=bias_all[:, cols], op=ADD
+                )
             nc.sync.dma_start(
                 out=out[b].rearrange("(p nb) d -> p nb d", nb=BLOCKS)[:, nb, :], in_=result[:]
             )

from contextlib import ExitStack

import concourse.mybir as mybir
from concourse.masks import make_identity

FLOPS = 2 * 2 * 1024 * 512 * 512 + 2 * 2 * 1024 * 512 * 1024

FP8X4 = mybir.dt.float8_e4m3fn_x4
BF16 = mybir.dt.bfloat16
F32 = mybir.dt.float32
I32 = mybir.dt.int32
U32 = mybir.dt.uint32
U8 = mybir.dt.uint8
ADD = mybir.AluOpType.add

P = 128
PACK = 4
SAMPLES = 2
TOKENS = 1024
MEM = 512
FEAT = 1024
BANKS = 8
BLOCKS = TOKENS // P
HALF = 512
BANK_SETS = 2
SET_BANKS = BANKS // BANK_SETS
ROW_GROUPS = P // SET_BANKS
ROWS = MEM // ROW_GROUPS
CHUNKS = ROWS // PACK
HALF_BLOCKS = BLOCKS // 2


def tile_proceduralmemory_pc_kernel(
    tc, pre, W_pm, proj_out_w_words, proj_out_w_scales, proj_out_b, out
):
    nc = tc.nc
    with ExitStack() as ctx:
        ctx.enter_context(tc.manual_schedule())
        consts = ctx.enter_context(tc.tile_pool(name="consts", bufs=1))
        sample = ctx.enter_context(tc.tile_pool(name="sample", bufs=SAMPLES))
        halves = ctx.enter_context(tc.tile_pool(name="halves", bufs=2 * SAMPLES))
        banks = ctx.enter_context(tc.tile_pool(name="banks", bufs=SAMPLES * CHUNKS))
        work = ctx.enter_context(tc.tile_pool(name="work", bufs=4))
        results = ctx.enter_context(tc.tile_pool(name="results", bufs=SAMPLES * BLOCKS))
        psum_early = ctx.enter_context(tc.psum_pool(name="psum_early", bufs=2))
        psum_post = ctx.enter_context(tc.psum_pool(name="psum_post", bufs=2))
        psum_product = ctx.enter_context(tc.psum_pool(name="psum_product", bufs=4))

        ones = consts.tile([P, P], BF16)
        nc.vector.memset(ones[:], 1.0)
        bias_row = consts.tile([P, FEAT], BF16)
        nc.vector.memset(bias_row[:], 0.0)
        bias_all = consts.tile([P, FEAT], F32)
        w_words = consts.tile([P, FEAT], U32, align_bytes=64)
        w_scales = consts.tile([P, FEAT], U8, align_bytes=64)
        nc.vector.memset(w_scales[:].bitcast(I32), 0)
        ident = consts.tile([P, P], BF16)
        make_identity(nc, ident[:])
        fold_f32 = consts.tile([P, ROW_GROUPS], F32)
        nc.vector.tensor_reduce(
            out=fold_f32[:],
            in_=ident[:].rearrange("q (k r) -> q r k", r=ROW_GROUPS),
            axis=mybir.AxisListType.X,
            op=ADD,
        )
        fold = consts.tile([P, ROW_GROUPS], BF16)
        nc.vector.tensor_copy(out=fold[:], in_=fold_f32[:])

        pre_rows = {}
        bank_rows = {}

        def load_tokens(b):
            tokens_view = pre[b].rearrange("(p nb) j -> p nb j", nb=BLOCKS)
            for half in range(2):
                pre_tile = halves.tile([P, HALF_BLOCKS, MEM], BF16)
                nc.sync.dma_start(
                    out=pre_tile[:],
                    in_=tokens_view[:, half * HALF_BLOCKS : (half + 1) * HALF_BLOCKS, :],
                )
                pre_rows[(b, half)] = pre_tile

        def load_banks(b):
            rows_view = W_pm[b].rearrange(
                "(h k) (r s) j -> (k r) h s j", h=BANK_SETS, s=ROWS
            )
            for c in range(CHUNKS):
                chunk_tile = banks.tile([P, BANK_SETS, PACK, MEM], BF16)
                nc.sync.dma_start(
                    out=chunk_tile[:], in_=rows_view[:, :, c * PACK : (c + 1) * PACK, :]
                )
                bank_rows[(b, c)] = chunk_tile

        load_tokens(0)
        nc.sync.dma_start(
            out=bias_row[0:1, :], in_=proj_out_b.rearrange("(o d) -> o d", o=1)
        )
        load_banks(0)
        nc.sync.dma_start(
            out=w_words[:].bitcast(I32),
            in_=proj_out_w_words[0].rearrange("p n t -> p (n t)").bitcast(I32),
        )
        for quadrant in range(4):
            nc.sync.dma_start(
                out=w_scales[32 * quadrant : 32 * quadrant + 4, :].bitcast(I32),
                in_=proj_out_w_scales[0, 4 * quadrant : 4 * quadrant + 4, :].bitcast(I32),
            )
        load_tokens(1)
        load_banks(1)

        pre_codes = {}
        pre_scales = {}
        wsum_grouped = {}
        wsum_codes = {}
        wsum_scales = {}
        for b in range(SAMPLES):
            codes = sample.tile([P, TOKENS], U32, align_bytes=64)
            scales = sample.tile([P, TOKENS], U8, align_bytes=64)
            grouped_sums = sample.tile(
                [P, PACK, ROW_GROUPS, CHUNKS, PACK], BF16, align_bytes=64
            )
            codes_w = sample.tile([P, MEM], U32, align_bytes=64)
            scales_w = sample.tile([P, MEM], U8, align_bytes=64)
            pre_codes[b] = codes
            pre_scales[b] = scales
            wsum_grouped[b] = grouped_sums
            wsum_codes[b] = codes_w
            wsum_scales[b] = scales_w

        def quantise_tokens(b, half):
            grouped = halves.tile([P, HALF_BLOCKS, P, PACK], BF16, align_bytes=64)
            for nb in range(HALF_BLOCKS):
                flipped = psum_early.tile([P, PACK, P], BF16, tag="early")
                for t in range(PACK):
                    nc.tensor.transpose(
                        out=flipped[:, t, :],
                        in_=pre_rows[(b, half)][:, nb, t * P : (t + 1) * P],
                        identity=ident[:],
                    )
                copy = nc.scalar.copy if nb % 2 == 0 else nc.vector.tensor_copy
                copy(out=grouped[:, nb, :, :], in_=flipped[:].rearrange("p t n -> p n t"))
            cols = slice(half * HALF_BLOCKS * P, (half + 1) * HALF_BLOCKS * P)
            nc.vector.quantize_mx(
                out=pre_codes[b][:, cols].bitcast(FP8X4),
                scales=pre_scales[b][:, cols],
                in_=grouped[:].rearrange("p nb n t -> p (nb n t)"),
            )

        def sum_banks(b, c):
            sums = psum_early.tile([P, PACK, ROW_GROUPS, PACK], F32, tag="early")
            for T in range(PACK):
                for t in range(PACK):
                    for h in range(BANK_SETS):
                        nc.tensor.matmul(
                            out=sums[:, T, :, t],
                            lhsT=bank_rows[(b, c)][:, h, T, t * P : (t + 1) * P],
                            rhs=fold[:],
                            start=(h == 0),
                            stop=(h == BANK_SETS - 1),
                        )
            nc.scalar.copy(
                out=wsum_grouped[b][:].rearrange("p T r c t -> p (T r) c t")[:, :, c, :],
                in_=sums[:].rearrange("p T r t -> p (T r) t"),
            )

        def quantise_bank_sums(b):
            nc.vector.quantize_mx(
                out=wsum_codes[b][:].bitcast(FP8X4),
                scales=wsum_scales[b][:],
                in_=wsum_grouped[b][:].rearrange("p T r c t -> p (T r c t)"),
            )

        def spread_bias():
            for h in range(FEAT // HALF):
                cols = slice(h * HALF, (h + 1) * HALF)
                product = psum_product.tile([P, HALF], F32)
                nc.tensor.matmul(
                    out=product[:], lhsT=ones[:], rhs=bias_row[:, cols], start=True, stop=True
                )
                nc.scalar.copy(out=bias_all[:, cols], in_=product[:])

        post_grouped = {}
        post_codes = {}
        post_scales = {}
        products = {}

        def first_product(g):
            b, nb = divmod(g, BLOCKS)
            post = psum_post.tile([P, PACK, P], F32)
            tokens = slice(nb * P, (nb + 1) * P)
            for T in range(PACK):
                rows = slice(T * P, (T + 1) * P)
                nc.tensor.matmul_mx(
                    out=post[:, T, :],
                    lhsT=wsum_codes[b][:, rows].bitcast(FP8X4),
                    lhsT_scale=wsum_scales[b][:, rows],
                    rhs=pre_codes[b][:, tokens].bitcast(FP8X4),
                    rhs_scale=pre_scales[b][:, tokens],
                    start=True,
                    stop=True,
                )
            grouped_post = work.tile([P, P, PACK], BF16, align_bytes=64)
            nc.scalar.copy(out=grouped_post[:], in_=post[:].rearrange("p T n -> p n T"))
            post_grouped[g] = grouped_post

        def quantise_post(g):
            codes_p = work.tile([P, P], U32, align_bytes=64)
            scales_p = work.tile([P, P], U8, align_bytes=64)
            nc.vector.quantize_mx(
                out=codes_p[:].bitcast(FP8X4),
                scales=scales_p[:],
                in_=post_grouped[g][:].rearrange("p n T -> p (n T)"),
            )
            post_codes[g] = codes_p
            post_scales[g] = scales_p

        def second_product(g):
            for h in range(FEAT // HALF):
                cols = slice(h * HALF, (h + 1) * HALF)
                product = psum_product.tile([P, HALF], F32)
                nc.tensor.matmul_mx(
                    out=product[:],
                    lhsT=post_codes[g][:].bitcast(FP8X4),
                    lhsT_scale=post_scales[g][:],
                    rhs=w_words[:, cols].bitcast(FP8X4),
                    rhs_scale=w_scales[:, cols],
                    start=True,
                    stop=True,
                )
                products[(g, h)] = product

        def add_bias_and_store(g):
            b, nb = divmod(g, BLOCKS)
            result = results.tile([P, FEAT], F32)
            for h in range(FEAT // HALF):
                cols = slice(h * HALF, (h + 1) * HALF)
                nc.vector.tensor_tensor(
                    out=result[:, cols], in0=products[(g, h)][:], in1=bias_all[:, cols], op=ADD
                )
            nc.sync.dma_start(
                out=out[b].rearrange("(p nb) d -> p nb d", nb=BLOCKS)[:, nb, :], in_=result[:]
            )

        quantise_tokens(0, 0)
        quantise_tokens(0, 1)
        for c in range(CHUNKS):
            sum_banks(0, c)
        quantise_bank_sums(0)
        spread_bias()

        n_blocks = SAMPLES * BLOCKS
        for step in range(-2, n_blocks):
            if step + 2 < n_blocks:
                first_product(step + 2)
            if 0 <= step + 1 < n_blocks:
                second_product(step + 1)
            if step >= 0:
                add_bias_and_store(step)
            if step + 2 < n_blocks:
                quantise_post(step + 2)
            if step < 0:
                quantise_tokens(1, step + 2)
            elif step < CHUNKS:
                sum_banks(1, step)
            elif step == CHUNKS:
                quantise_bank_sums(1)
